import numpy as np
import ml_dtypes

BF16 = ml_dtypes.bfloat16


def bf(x):
    return np.asarray(x, np.float32).astype(BF16)


def f32(x):
    return np.asarray(x, np.float32)


def f64(x):
    return np.asarray(x).astype(np.float64)


def striped(idx):
    return np.tile(idx.reshape(-1, 16).T, (8, 1))


C, S, N, D0, D1, TAPS = 256, 4096, 4096, 2, 4, 2


def butterfly(v, w, d):
    h = d // TAPS
    vb = v.reshape(v.shape[0], -1, d)
    v0, v1 = vb[..., :h], vb[..., h:]
    top = w[0, :h] * v0 + w[1, :h] * v1
    bot = w[0, h:] * v0 + w[1, h:] * v1
    return np.concatenate([top, bot], axis=-1).reshape(v.shape)


def setup_inputs():
    hann = 0.5 - 0.5 * np.cos(2.0 * np.pi * np.arange(S) / S)
    return {"x": f32(np.random.standard_normal((C, S))), "win": f32((hann + 0.1 * np.random.standard_normal(S)).reshape(1, S)), "rw0": f32(0.5 * np.random.standard_normal((TAPS, D0))), "iw0": f32(0.5 * np.random.standard_normal((TAPS, D0))), "rw1": f32(0.5 * np.random.standard_normal((TAPS, D1))), "iw1": f32(0.5 * np.random.standard_normal((TAPS, D1))), "offs": striped(np.random.permutation(S)[:N])}


def reference(x, win, rw0, iw0, rw1, iw1, offs):
    idx = offs[:16].T.reshape(-1)
    r0 = (f64(x) * f64(win))[:, idx]
    r1 = butterfly(r0, f64(rw0), D0)
    i1 = butterfly(r0, f64(iw0), D0)
    return butterfly(r1, f64(rw1), D1) - butterfly(i1, f64(iw1), D1)

@@ -1,0 +1,84 @@
+import concourse.mybir as mybir
+
+F32 = mybir.dt.float32
+U16 = mybir.dt.uint16
+MULT = mybir.AluOpType.mult
+ADD = mybir.AluOpType.add
+COPY = mybir.ActivationFunctionType.Copy
+
+P = 128
+C = 256
+S = 4096
+TAPS = 4
+PIECE = 2048
+GROUPS = PIECE // TAPS
+
+FLOPS = C * S * (1 + 2 * TAPS - 1)
+
+
+def load_for_all_partitions(nc, pool, source, name):
+    rows, cols = source.shape
+    tile = pool.tile([P, rows * cols], F32, name=name)
+    nc.sync.dma_start(tile[:], source.rearrange("r c -> (r c)").partition_broadcast(P))
+    return tile
+
+
+def make_mix(nc, pool, rw0, iw0, rw1, iw1):
+    stage_one = {"re": load_for_all_partitions(nc, pool, rw0, "rw0_all"), "im": load_for_all_partitions(nc, pool, iw0, "iw0_all")}
+    stage_two = {"re": load_for_all_partitions(nc, pool, rw1, "rw1_all"), "im": load_for_all_partitions(nc, pool, iw1, "iw1_all")}
+    products = {}
+    for part in ("re", "im"):
+        products[part] = pool.tile([P, TAPS * TAPS], F32, name="products_" + part)
+        by_a_b = products[part][:].rearrange("c (a b h q) -> c a b h q", a=2, b=2, h=2)
+        second = stage_two[part][:].rearrange("c (a h q) -> c a h q", a=2, h=2)
+        for b in range(2):
+            first = stage_one[part][:, 2 * b : 2 * b + 2].unsqueeze(1).unsqueeze(1).to_broadcast([P, 2, 2, 2])
+            nc.vector.tensor_tensor(by_a_b[:, :, b, :, :], second, first, MULT)
+    mix = pool.tile([P, TAPS * TAPS], F32, name="mix")
+    nc.vector.tensor_sub(mix[:], products["re"][:], products["im"][:])
+    return mix
+
+
+def tile_tfft_kernel(tc, x, win, rw0, iw0, rw1, iw1, offs, out):
+    nc = tc.nc
+    with (
+        tc.tile_pool(name="held", bufs=1) as held,
+        tc.tile_pool(name="loads", bufs=2) as loads,
+        tc.tile_pool(name="work", bufs=2) as work,
+    ):
+        offsets = held.tile([P, S // 16], U16, name="offsets")
+        nc.sync.dma_start(offsets[:], offs)
+        taper = held.tile([P, S], F32, name="taper")
+        nc.scalar.dma_start(taper[:], win.rearrange("o s -> (o s)").partition_broadcast(P))
+        mix = make_mix(nc, held, rw0, iw0, rw1, iw1)
+
+        for block in range(C // P):
+            frames = x[block * P : (block + 1) * P, :]
+            raw = loads.tile([P, S], F32, name="raw")
+            nc.sync.dma_start(raw[:], frames)
+            y = held.tile([P, S], F32, name="y" + str(block))
+            nc.vector.tensor_mul(y[:], raw[:], taper[:])
+
+            for piece in range(S // PIECE):
+                listed = offsets[:, piece * (PIECE // 16) : (piece + 1) * (PIECE // 16)]
+                r0 = work.tile([P, PIECE], F32, name="r0")
+                nc.scalar.activation(r0[:], y[:].indirect(listed), COPY)
+                tap = r0[:].rearrange("c (u k) -> c k u", k=TAPS)
+
+                halves = [work.tile([P, PIECE], F32, name="half" + str(i)) for i in range(2)]
+                for i in range(2):
+                    for p in range(TAPS):
+                        plane = halves[i][:, p * GROUPS : (p + 1) * GROUPS]
+                        even = TAPS * (2 * i) + p
+                        odd = TAPS * (2 * i + 1) + p
+                        nc.vector.tensor_scalar_mul(plane, tap[:, 2 * i, :], mix[:, even : even + 1])
+                        nc.vector.scalar_tensor_tensor(plane, tap[:, 2 * i + 1, :], mix[:, odd : odd + 1], plane, MULT, ADD)
+
+                result = work.tile([P, PIECE], F32, name="result")
+                nc.vector.tensor_tensor(
+                    result[:].rearrange("c (u p) -> c u p", p=TAPS),
+                    halves[0][:].rearrange("c (p u) -> c u p", p=TAPS),
+                    halves[1][:].rearrange("c (p u) -> c u p", p=TAPS),
+                    ADD,
+                )
+                nc.sync.dma_start(out[block * P : (block + 1) * P, piece * PIECE : (piece + 1) * PIECE], result[:])

@@ -1,4 +1,5 @@
 import concourse.mybir as mybir
+from concourse.masks import make_identity
 
 F32 = mybir.dt.float32
 U16 = mybir.dt.uint16
@@ -9,11 +10,12 @@ COPY = mybir.ActivationFunctionType.Copy
 P = 128
 C = 256
 S = 4096
-TAPS = 4
-PIECE = 2048
-GROUPS = PIECE // TAPS
+QUAD = 4
+PIECE = 512
+SQUARES = PIECE // P
+CHUNK = 1024
 
-FLOPS = C * S * (1 + 2 * TAPS - 1)
+FLOPS = C * S * (1 + 2 * QUAD - 1)
 
 
 def load_for_all_partitions(nc, pool, source, name):
@@ -28,57 +30,86 @@ def make_mix(nc, pool, rw0, iw0, rw1, iw1):
     stage_two = {"re": load_for_all_partitions(nc, pool, rw1, "rw1_all"), "im": load_for_all_partitions(nc, pool, iw1, "iw1_all")}
     products = {}
     for part in ("re", "im"):
-        products[part] = pool.tile([P, TAPS * TAPS], F32, name="products_" + part)
+        products[part] = pool.tile([P, QUAD * QUAD], F32, name="products_" + part)
         by_a_b = products[part][:].rearrange("c (a b h q) -> c a b h q", a=2, b=2, h=2)
         second = stage_two[part][:].rearrange("c (a h q) -> c a h q", a=2, h=2)
         for b in range(2):
             first = stage_one[part][:, 2 * b : 2 * b + 2].unsqueeze(1).unsqueeze(1).to_broadcast([P, 2, 2, 2])
             nc.vector.tensor_tensor(by_a_b[:, :, b, :, :], second, first, MULT)
-    mix = pool.tile([P, TAPS * TAPS], F32, name="mix")
+    mix = pool.tile([P, QUAD * QUAD], F32, name="mix")
     nc.vector.tensor_sub(mix[:], products["re"][:], products["im"][:])
     return mix
 
 
+def make_butterfly(nc, pool, identity, mix):
+    quads = P // QUAD
+    butterfly = pool.tile([P, P], F32, name="butterfly")
+    rows_of_tap = pool.tile([P, P], F32, name="rows_of_tap")
+    for k in range(QUAD):
+        target = butterfly if k == 0 else rows_of_tap
+        nc.vector.tensor_tensor(
+            target[:].rearrange("j (u p) -> j u p", p=QUAD),
+            identity[:].rearrange("j (u k) -> j u k", k=QUAD)[:, :, k : k + 1].to_broadcast([P, quads, QUAD]),
+            mix[:, QUAD * k : QUAD * (k + 1)].unsqueeze(1).to_broadcast([P, quads, QUAD]),
+            MULT,
+        )
+        if k > 0:
+            nc.vector.tensor_add(butterfly[:], butterfly[:], rows_of_tap[:])
+    return butterfly
+
+
 def tile_tfft_kernel(tc, x, win, rw0, iw0, rw1, iw1, offs, out):
     nc = tc.nc
+    blocks = C // P
+    pieces = [(block, piece) for block in range(blocks) for piece in range(S // PIECE)]
     with (
         tc.tile_pool(name="held", bufs=1) as held,
-        tc.tile_pool(name="loads", bufs=2) as loads,
-        tc.tile_pool(name="work", bufs=2) as work,
+        tc.tile_pool(name="work", bufs=4) as work,
+        tc.psum_pool(name="banks", bufs=4) as banks,
     ):
         offsets = held.tile([P, S // 16], U16, name="offsets")
         nc.sync.dma_start(offsets[:], offs)
+        identity = held.tile([P, P], F32, name="identity")
+        make_identity(nc, identity[:])
+        butterfly = make_butterfly(nc, held, identity, make_mix(nc, held, rw0, iw0, rw1, iw1))
+
         taper = held.tile([P, S], F32, name="taper")
-        nc.scalar.dma_start(taper[:], win.rearrange("o s -> (o s)").partition_broadcast(P))
-        mix = make_mix(nc, held, rw0, iw0, rw1, iw1)
-
-        for block in range(C // P):
-            frames = x[block * P : (block + 1) * P, :]
-            raw = loads.tile([P, S], F32, name="raw")
-            nc.sync.dma_start(raw[:], frames)
+        win_row = win.rearrange("o s -> (o s)")
+        windows = []
+        for block in range(blocks):
+            raw = held.tile([P, S], F32, name="raw" + str(block))
             y = held.tile([P, S], F32, name="y" + str(block))
-            nc.vector.tensor_mul(y[:], raw[:], taper[:])
+            engine = nc.vector if block == 0 else nc.gpsimd
+            for start in range(0, S, CHUNK):
+                if block == 0:
+                    nc.scalar.dma_start(taper[:, start : start + CHUNK], win_row[start : start + CHUNK].partition_broadcast(P))
+                nc.sync.dma_start(raw[:, start : start + CHUNK], x[block * P : (block + 1) * P, start : start + CHUNK])
+                engine.tensor_tensor(y[:, start : start + CHUNK], raw[:, start : start + CHUNK], taper[:, start : start + CHUNK], MULT)
+            windows.append(y)
 
-            for piece in range(S // PIECE):
-                listed = offsets[:, piece * (PIECE // 16) : (piece + 1) * (PIECE // 16)]
-                r0 = work.tile([P, PIECE], F32, name="r0")
-                nc.scalar.activation(r0[:], y[:].indirect(listed), COPY)
-                tap = r0[:].rearrange("c (u k) -> c k u", k=TAPS)
+        def look_up_and_flip(block, piece):
+            r0 = work.tile([P, PIECE], F32, name="r0")
+            listed = offsets[:, piece * (PIECE // 16) : (piece + 1) * (PIECE // 16)]
+            nc.scalar.activation(r0[:], windows[block][:].indirect(listed), COPY)
+            flipped_bank = banks.tile([P, PIECE], F32, name="flipped_bank")
+            for q in range(SQUARES):
+                nc.tensor.transpose(flipped_bank[:, q * P : (q + 1) * P], r0[:, q * P : (q + 1) * P], identity[:])
+            flipped = work.tile([P, PIECE], F32, name="flipped")
+            nc.vector.tensor_copy(flipped[:], flipped_bank[:])
+            return flipped
 
-                halves = [work.tile([P, PIECE], F32, name="half" + str(i)) for i in range(2)]
-                for i in range(2):
-                    for p in range(TAPS):
-                        plane = halves[i][:, p * GROUPS : (p + 1) * GROUPS]
-                        even = TAPS * (2 * i) + p
-                        odd = TAPS * (2 * i + 1) + p
-                        nc.vector.tensor_scalar_mul(plane, tap[:, 2 * i, :], mix[:, even : even + 1])
-                        nc.vector.scalar_tensor_tensor(plane, tap[:, 2 * i + 1, :], mix[:, odd : odd + 1], plane, MULT, ADD)
+        def mix_and_store(block, piece, flipped):
+            mixed_bank = banks.tile([P, PIECE], F32, name="mixed_bank")
+            for q in range(SQUARES):
+                nc.tensor.matmul(mixed_bank[:, q * P : (q + 1) * P], flipped[:, q * P : (q + 1) * P], butterfly[:], start=True, stop=True)
+            mixed = work.tile([P, PIECE], F32, name="mixed")
+            nc.vector.tensor_copy(mixed[:], mixed_bank[:])
+            nc.sync.dma_start(out[block * P : (block + 1) * P, piece * PIECE : (piece + 1) * PIECE], mixed[:])
 
-                result = work.tile([P, PIECE], F32, name="result")
-                nc.vector.tensor_tensor(
-                    result[:].rearrange("c (u p) -> c u p", p=TAPS),
-                    halves[0][:].rearrange("c (p u) -> c u p", p=TAPS),
-                    halves[1][:].rearrange("c (p u) -> c u p", p=TAPS),
-                    ADD,
-                )
-                nc.sync.dma_start(out[block * P : (block + 1) * P, piece * PIECE : (piece + 1) * PIECE], result[:])
+        waiting = None
+        for block, piece in pieces:
+            flipped = look_up_and_flip(block, piece)
+            if waiting is not None:
+                mix_and_store(*waiting)
+            waiting = (block, piece, flipped)
+        mix_and_store(*waiting)

@@ -4,7 +4,6 @@ from concourse.masks import make_identity
 F32 = mybir.dt.float32
 U16 = mybir.dt.uint16
 MULT = mybir.AluOpType.mult
-ADD = mybir.AluOpType.add
 COPY = mybir.ActivationFunctionType.Copy
 
 P = 128
@@ -12,7 +11,6 @@ C = 256
 S = 4096
 QUAD = 4
 PIECE = 512
-SQUARES = PIECE // P
 CHUNK = 1024
 
 FLOPS = C * S * (1 + 2 * QUAD - 1)
@@ -88,22 +86,18 @@ def tile_tfft_kernel(tc, x, win, rw0, iw0, rw1, iw1, offs, out):
             windows.append(y)
 
         def look_up_and_flip(block, piece):
-            r0 = work.tile([P, PIECE], F32, name="r0")
+            r0 = work.tile([P, PIECE], F32, name="r0", align_bytes=64)
             listed = offsets[:, piece * (PIECE // 16) : (piece + 1) * (PIECE // 16)]
             nc.scalar.activation(r0[:], windows[block][:].indirect(listed), COPY)
-            flipped_bank = banks.tile([P, PIECE], F32, name="flipped_bank")
-            for q in range(SQUARES):
-                nc.tensor.transpose(flipped_bank[:, q * P : (q + 1) * P], r0[:, q * P : (q + 1) * P], identity[:])
-            flipped = work.tile([P, PIECE], F32, name="flipped")
-            nc.vector.tensor_copy(flipped[:], flipped_bank[:])
+            flipped = work.tile([P, PIECE], F32, name="flipped", align_bytes=64)
+            nc.vector.transpose(flipped[:], r0[:])
             return flipped
 
         def mix_and_store(block, piece, flipped):
             mixed_bank = banks.tile([P, PIECE], F32, name="mixed_bank")
-            for q in range(SQUARES):
-                nc.tensor.matmul(mixed_bank[:, q * P : (q + 1) * P], flipped[:, q * P : (q + 1) * P], butterfly[:], start=True, stop=True)
-            mixed = work.tile([P, PIECE], F32, name="mixed")
-            nc.vector.tensor_copy(mixed[:], mixed_bank[:])
+            nc.tensor.matmul(mixed_bank[:], butterfly[:], flipped[:], start=True, stop=True)
+            mixed = work.tile([P, PIECE], F32, name="mixed", align_bytes=64)
+            nc.vector.transpose(mixed[:], mixed_bank[:])
             nc.sync.dma_start(out[block * P : (block + 1) * P, piece * PIECE : (piece + 1) * PIECE], mixed[:])
 
         waiting = None

@@ -77,12 +77,11 @@ def tile_tfft_kernel(tc, x, win, rw0, iw0, rw1, iw1, offs, out):
         for block in range(blocks):
             raw = held.tile([P, S], F32, name="raw" + str(block))
             y = held.tile([P, S], F32, name="y" + str(block))
-            engine = nc.vector if block == 0 else nc.gpsimd
             for start in range(0, S, CHUNK):
                 if block == 0:
                     nc.scalar.dma_start(taper[:, start : start + CHUNK], win_row[start : start + CHUNK].partition_broadcast(P))
                 nc.sync.dma_start(raw[:, start : start + CHUNK], x[block * P : (block + 1) * P, start : start + CHUNK])
-                engine.tensor_tensor(y[:, start : start + CHUNK], raw[:, start : start + CHUNK], taper[:, start : start + CHUNK], MULT)
+                nc.vector.tensor_tensor(y[:, start : start + CHUNK], raw[:, start : start + CHUNK], taper[:, start : start + CHUNK], MULT)
             windows.append(y)
 
         def look_up_and_flip(block, piece):

@@ -10,10 +10,20 @@ P = 128
 C = 256
 S = 4096
 QUAD = 4
-PIECE = 512
+BANK = 512
 CHUNK = 1024
 
 FLOPS = C * S * (1 + 2 * QUAD - 1)
+
+
+def halving_widths(total, least):
+    widths = []
+    left = total
+    while left > least:
+        widths.append(left // 2)
+        left -= left // 2
+    widths.append(left)
+    return widths
 
 
 def load_for_all_partitions(nc, pool, source, name):
@@ -59,7 +69,8 @@ def make_butterfly(nc, pool, identity, mix):
 def tile_tfft_kernel(tc, x, win, rw0, iw0, rw1, iw1, offs, out):
     nc = tc.nc
     blocks = C // P
-    pieces = [(block, piece) for block in range(blocks) for piece in range(S // PIECE)]
+    widths = halving_widths(S, BANK)
+    pieces = [(block, sum(widths[:i]), widths[i]) for block in range(blocks) for i in range(len(widths))]
     with (
         tc.tile_pool(name="held", bufs=1) as held,
         tc.tile_pool(name="work", bufs=4) as work,
@@ -84,25 +95,26 @@ def tile_tfft_kernel(tc, x, win, rw0, iw0, rw1, iw1, offs, out):
                 nc.vector.tensor_tensor(y[:, start : start + CHUNK], raw[:, start : start + CHUNK], taper[:, start : start + CHUNK], MULT)
             windows.append(y)
 
-        def look_up_and_flip(block, piece):
-            r0 = work.tile([P, PIECE], F32, name="r0", align_bytes=64)
-            listed = offsets[:, piece * (PIECE // 16) : (piece + 1) * (PIECE // 16)]
+        def look_up_and_flip(block, start, width):
+            r0 = work.tile([P, width], F32, name="r0", align_bytes=64)
+            listed = offsets[:, start // 16 : (start + width) // 16]
             nc.scalar.activation(r0[:], windows[block][:].indirect(listed), COPY)
-            flipped = work.tile([P, PIECE], F32, name="flipped", align_bytes=64)
+            flipped = work.tile([P, width], F32, name="flipped", align_bytes=64)
             nc.vector.transpose(flipped[:], r0[:])
             return flipped
 
-        def mix_and_store(block, piece, flipped):
-            mixed_bank = banks.tile([P, PIECE], F32, name="mixed_bank")
-            nc.tensor.matmul(mixed_bank[:], butterfly[:], flipped[:], start=True, stop=True)
-            mixed = work.tile([P, PIECE], F32, name="mixed", align_bytes=64)
-            nc.vector.transpose(mixed[:], mixed_bank[:])
-            nc.sync.dma_start(out[block * P : (block + 1) * P, piece * PIECE : (piece + 1) * PIECE], mixed[:])
+        def mix_and_store(block, start, width, flipped):
+            for part in range(0, width, BANK):
+                mixed_bank = banks.tile([P, BANK], F32, name="mixed_bank")
+                nc.tensor.matmul(mixed_bank[:], butterfly[:], flipped[:, part : part + BANK], start=True, stop=True)
+                mixed = work.tile([P, BANK], F32, name="mixed", align_bytes=64)
+                nc.vector.transpose(mixed[:], mixed_bank[:])
+                nc.sync.dma_start(out[block * P : (block + 1) * P, start + part : start + part + BANK], mixed[:])
 
         waiting = None
-        for block, piece in pieces:
-            flipped = look_up_and_flip(block, piece)
+        for block, start, width in pieces:
+            flipped = look_up_and_flip(block, start, width)
             if waiting is not None:
                 mix_and_store(*waiting)
-            waiting = (block, piece, flipped)
+            waiting = (block, start, width, flipped)
         mix_and_store(*waiting)

@@ -10,20 +10,11 @@ P = 128
 C = 256
 S = 4096
 QUAD = 4
-BANK = 512
+PIECE = 512
 CHUNK = 1024
+WARM_UPS = 2
 
 FLOPS = C * S * (1 + 2 * QUAD - 1)
-
-
-def halving_widths(total, least):
-    widths = []
-    left = total
-    while left > least:
-        widths.append(left // 2)
-        left -= left // 2
-    widths.append(left)
-    return widths
 
 
 def load_for_all_partitions(nc, pool, source, name):
@@ -69,8 +60,7 @@ def make_butterfly(nc, pool, identity, mix):
 def tile_tfft_kernel(tc, x, win, rw0, iw0, rw1, iw1, offs, out):
     nc = tc.nc
     blocks = C // P
-    widths = halving_widths(S, BANK)
-    pieces = [(block, sum(widths[:i]), widths[i]) for block in range(blocks) for i in range(len(widths))]
+    pieces = [(block, piece) for block in range(blocks) for piece in range(S // PIECE)]
     with (
         tc.tile_pool(name="held", bufs=1) as held,
         tc.tile_pool(name="work", bufs=4) as work,
@@ -95,26 +85,29 @@ def tile_tfft_kernel(tc, x, win, rw0, iw0, rw1, iw1, offs, out):
                 nc.vector.tensor_tensor(y[:, start : start + CHUNK], raw[:, start : start + CHUNK], taper[:, start : start + CHUNK], MULT)
             windows.append(y)
 
-        def look_up_and_flip(block, start, width):
-            r0 = work.tile([P, width], F32, name="r0", align_bytes=64)
-            listed = offsets[:, start // 16 : (start + width) // 16]
+        for warm_up in range(WARM_UPS):
+            unread_bank = banks.tile([P, PIECE], F32, name="unread_bank")
+            nc.tensor.matmul(unread_bank[:], butterfly[:], windows[0][:, S - PIECE : S], start=True, stop=True)
+
+        def look_up_and_flip(block, piece):
+            r0 = work.tile([P, PIECE], F32, name="r0", align_bytes=64)
+            listed = offsets[:, piece * (PIECE // 16) : (piece + 1) * (PIECE // 16)]
             nc.scalar.activation(r0[:], windows[block][:].indirect(listed), COPY)
-            flipped = work.tile([P, width], F32, name="flipped", align_bytes=64)
+            flipped = work.tile([P, PIECE], F32, name="flipped", align_bytes=64)
             nc.vector.transpose(flipped[:], r0[:])
             return flipped
 
-        def mix_and_store(block, start, width, flipped):
-            for part in range(0, width, BANK):
-                mixed_bank = banks.tile([P, BANK], F32, name="mixed_bank")
-                nc.tensor.matmul(mixed_bank[:], butterfly[:], flipped[:, part : part + BANK], start=True, stop=True)
-                mixed = work.tile([P, BANK], F32, name="mixed", align_bytes=64)
-                nc.vector.transpose(mixed[:], mixed_bank[:])
-                nc.sync.dma_start(out[block * P : (block + 1) * P, start + part : start + part + BANK], mixed[:])
+        def mix_and_store(block, piece, flipped):
+            mixed_bank = banks.tile([P, PIECE], F32, name="mixed_bank")
+            nc.tensor.matmul(mixed_bank[:], butterfly[:], flipped[:], start=True, stop=True)
+            mixed = work.tile([P, PIECE], F32, name="mixed", align_bytes=64)
+            nc.vector.transpose(mixed[:], mixed_bank[:])
+            nc.sync.dma_start(out[block * P : (block + 1) * P, piece * PIECE : (piece + 1) * PIECE], mixed[:])
 
         waiting = None
-        for block, start, width in pieces:
-            flipped = look_up_and_flip(block, start, width)
+        for block, piece in pieces:
+            flipped = look_up_and_flip(block, piece)
             if waiting is not None:
                 mix_and_store(*waiting)
-            waiting = (block, start, width, flipped)
+            waiting = (block, piece, flipped)
         mix_and_store(*waiting)

@@ -12,7 +12,6 @@ S = 4096
 QUAD = 4
 PIECE = 512
 CHUNK = 1024
-WARM_UPS = 2
 
 FLOPS = C * S * (1 + 2 * QUAD - 1)
 
@@ -34,9 +33,9 @@ def make_mix(nc, pool, rw0, iw0, rw1, iw1):
         second = stage_two[part][:].rearrange("c (a h q) -> c a h q", a=2, h=2)
         for b in range(2):
             first = stage_one[part][:, 2 * b : 2 * b + 2].unsqueeze(1).unsqueeze(1).to_broadcast([P, 2, 2, 2])
-            nc.vector.tensor_tensor(by_a_b[:, :, b, :, :], second, first, MULT)
+            nc.gpsimd.tensor_tensor(by_a_b[:, :, b, :, :], second, first, MULT)
     mix = pool.tile([P, QUAD * QUAD], F32, name="mix")
-    nc.vector.tensor_sub(mix[:], products["re"][:], products["im"][:])
+    nc.gpsimd.tensor_sub(mix[:], products["re"][:], products["im"][:])
     return mix
 
 
@@ -46,14 +45,14 @@ def make_butterfly(nc, pool, identity, mix):
     rows_of_tap = pool.tile([P, P], F32, name="rows_of_tap")
     for k in range(QUAD):
         target = butterfly if k == 0 else rows_of_tap
-        nc.vector.tensor_tensor(
+        nc.gpsimd.tensor_tensor(
             target[:].rearrange("j (u p) -> j u p", p=QUAD),
             identity[:].rearrange("j (u k) -> j u k", k=QUAD)[:, :, k : k + 1].to_broadcast([P, quads, QUAD]),
             mix[:, QUAD * k : QUAD * (k + 1)].unsqueeze(1).to_broadcast([P, quads, QUAD]),
             MULT,
         )
         if k > 0:
-            nc.vector.tensor_add(butterfly[:], butterfly[:], rows_of_tap[:])
+            nc.gpsimd.tensor_add(butterfly[:], butterfly[:], rows_of_tap[:])
     return butterfly
 
 
@@ -66,11 +65,11 @@ def tile_tfft_kernel(tc, x, win, rw0, iw0, rw1, iw1, offs, out):
         tc.tile_pool(name="work", bufs=4) as work,
         tc.psum_pool(name="banks", bufs=4) as banks,
     ):
-        offsets = held.tile([P, S // 16], U16, name="offsets")
-        nc.sync.dma_start(offsets[:], offs)
         identity = held.tile([P, P], F32, name="identity")
         make_identity(nc, identity[:])
         butterfly = make_butterfly(nc, held, identity, make_mix(nc, held, rw0, iw0, rw1, iw1))
+        offsets = held.tile([P, S // 16], U16, name="offsets")
+        nc.sync.dma_start(offsets[:], offs)
 
         taper = held.tile([P, S], F32, name="taper")
         win_row = win.rearrange("o s -> (o s)")
@@ -84,10 +83,6 @@ def tile_tfft_kernel(tc, x, win, rw0, iw0, rw1, iw1, offs, out):
                 nc.sync.dma_start(raw[:, start : start + CHUNK], x[block * P : (block + 1) * P, start : start + CHUNK])
                 nc.vector.tensor_tensor(y[:, start : start + CHUNK], raw[:, start : start + CHUNK], taper[:, start : start + CHUNK], MULT)
             windows.append(y)
-
-        for warm_up in range(WARM_UPS):
-            unread_bank = banks.tile([P, PIECE], F32, name="unread_bank")
-            nc.tensor.matmul(unread_bank[:], butterfly[:], windows[0][:, S - PIECE : S], start=True, stop=True)
 
         def look_up_and_flip(block, piece):
             r0 = work.tile([P, PIECE], F32, name="r0", align_bytes=64)

@@ -19,7 +19,7 @@ FLOPS = C * S * (1 + 2 * QUAD - 1)
 def load_for_all_partitions(nc, pool, source, name):
     rows, cols = source.shape
     tile = pool.tile([P, rows * cols], F32, name=name)
-    nc.sync.dma_start(tile[:], source.rearrange("r c -> (r c)").partition_broadcast(P))
+    nc.scalar.dma_start(tile[:], source.rearrange("r c -> (r c)").partition_broadcast(P))
     return tile
 
 
@@ -68,20 +68,38 @@ def tile_tfft_kernel(tc, x, win, rw0, iw0, rw1, iw1, offs, out):
         identity = held.tile([P, P], F32, name="identity")
         make_identity(nc, identity[:])
         butterfly = make_butterfly(nc, held, identity, make_mix(nc, held, rw0, iw0, rw1, iw1))
-        offsets = held.tile([P, S // 16], U16, name="offsets")
-        nc.sync.dma_start(offsets[:], offs)
 
+        win_quads = held.tile([P, S // P], F32, name="win_quads")
+        nc.sync.dma_start(
+            win_quads[:].rearrange("p (g e) -> p g e", e=QUAD),
+            win.rearrange("o (g p e) -> p (o g) e", p=P, e=QUAD),
+        )
+
+        def spread_taper(start):
+            taper_bank = banks.tile([P, PIECE], F32, name="mixed_bank")
+            every_fourth = taper_bank[:].rearrange("c (p e) -> c p e", e=QUAD)
+            for e in range(QUAD):
+                column = QUAD * (start // PIECE) + e
+                nc.tensor.transpose(every_fourth[:, :, e], win_quads[:, column : column + 1].to_broadcast([P, P]), identity[:])
+            return taper_bank
+
+        offsets = held.tile([P, S // 16], U16, name="offsets")
         taper = held.tile([P, S], F32, name="taper")
-        win_row = win.rearrange("o s -> (o s)")
         windows = []
         for block in range(blocks):
             raw = held.tile([P, S], F32, name="raw" + str(block))
             y = held.tile([P, S], F32, name="y" + str(block))
             for start in range(0, S, CHUNK):
-                if block == 0:
-                    nc.scalar.dma_start(taper[:, start : start + CHUNK], win_row[start : start + CHUNK].partition_broadcast(P))
                 nc.sync.dma_start(raw[:, start : start + CHUNK], x[block * P : (block + 1) * P, start : start + CHUNK])
-                nc.vector.tensor_tensor(y[:, start : start + CHUNK], raw[:, start : start + CHUNK], taper[:, start : start + CHUNK], MULT)
+                if block == 0:
+                    for part in range(start, start + CHUNK, PIECE):
+                        taper_bank = spread_taper(part)
+                        nc.vector.tensor_tensor(y[:, part : part + PIECE], raw[:, part : part + PIECE], taper_bank[:], MULT)
+                        nc.scalar.copy(taper[:, part : part + PIECE], taper_bank[:])
+                else:
+                    nc.vector.tensor_tensor(y[:, start : start + CHUNK], raw[:, start : start + CHUNK], taper[:, start : start + CHUNK], MULT)
+            if block == 0:
+                nc.sync.dma_start(offsets[:], offs)
             windows.append(y)
 
         def look_up_and_flip(block, piece):

@@ -97,7 +97,7 @@ def tile_tfft_kernel(tc, x, win, rw0, iw0, rw1, iw1, offs, out):
                         nc.vector.tensor_tensor(y[:, part : part + PIECE], raw[:, part : part + PIECE], taper_bank[:], MULT)
                         nc.scalar.copy(taper[:, part : part + PIECE], taper_bank[:])
                 else:
-                    nc.vector.tensor_tensor(y[:, start : start + CHUNK], raw[:, start : start + CHUNK], taper[:, start : start + CHUNK], MULT)
+                    nc.gpsimd.tensor_tensor(y[:, start : start + CHUNK], raw[:, start : start + CHUNK], taper[:, start : start + CHUNK], MULT)
             if block == 0:
                 nc.sync.dma_start(offsets[:], offs)
             windows.append(y)

@@ -16,16 +16,16 @@ CHUNK = 1024
 FLOPS = C * S * (1 + 2 * QUAD - 1)
 
 
-def load_for_all_partitions(nc, pool, source, name):
+def load_for_all_partitions(queue, pool, source, name):
     rows, cols = source.shape
     tile = pool.tile([P, rows * cols], F32, name=name)
-    nc.scalar.dma_start(tile[:], source.rearrange("r c -> (r c)").partition_broadcast(P))
+    queue.dma_start(tile[:], source.rearrange("r c -> (r c)").partition_broadcast(P))
     return tile
 
 
 def make_mix(nc, pool, rw0, iw0, rw1, iw1):
-    stage_one = {"re": load_for_all_partitions(nc, pool, rw0, "rw0_all"), "im": load_for_all_partitions(nc, pool, iw0, "iw0_all")}
-    stage_two = {"re": load_for_all_partitions(nc, pool, rw1, "rw1_all"), "im": load_for_all_partitions(nc, pool, iw1, "iw1_all")}
+    stage_one = {"re": load_for_all_partitions(nc.sync, pool, rw0, "rw0_all"), "im": load_for_all_partitions(nc.scalar, pool, iw0, "iw0_all")}
+    stage_two = {"re": load_for_all_partitions(nc.sync, pool, rw1, "rw1_all"), "im": load_for_all_partitions(nc.scalar, pool, iw1, "iw1_all")}
     products = {}
     for part in ("re", "im"):
         products[part] = pool.tile([P, QUAD * QUAD], F32, name="products_" + part)

@@ -11,7 +11,7 @@ C = 256
 S = 4096
 QUAD = 4
 PIECE = 512
-CHUNK = 1024
+CHUNK = 512
 
 FLOPS = C * S * (1 + 2 * QUAD - 1)
 
@@ -63,7 +63,7 @@ def tile_tfft_kernel(tc, x, win, rw0, iw0, rw1, iw1, offs, out):
     with (
         tc.tile_pool(name="held", bufs=1) as held,
         tc.tile_pool(name="work", bufs=4) as work,
-        tc.psum_pool(name="banks", bufs=4) as banks,
+        tc.psum_pool(name="banks", bufs=8) as banks,
     ):
         identity = held.tile([P, P], F32, name="identity")
         make_identity(nc, identity[:])
@@ -85,6 +85,7 @@ def tile_tfft_kernel(tc, x, win, rw0, iw0, rw1, iw1, offs, out):
 
         offsets = held.tile([P, S // 16], U16, name="offsets")
         taper = held.tile([P, S], F32, name="taper")
+        taper_banks = {}
         windows = []
         for block in range(blocks):
             raw = held.tile([P, S], F32, name="raw" + str(block))
@@ -93,12 +94,14 @@ def tile_tfft_kernel(tc, x, win, rw0, iw0, rw1, iw1, offs, out):
                 nc.sync.dma_start(raw[:, start : start + CHUNK], x[block * P : (block + 1) * P, start : start + CHUNK])
                 if block == 0:
                     for part in range(start, start + CHUNK, PIECE):
-                        taper_bank = spread_taper(part)
-                        nc.vector.tensor_tensor(y[:, part : part + PIECE], raw[:, part : part + PIECE], taper_bank[:], MULT)
-                        nc.scalar.copy(taper[:, part : part + PIECE], taper_bank[:])
+                        taper_banks[part] = spread_taper(part)
+                        if part > 0:
+                            nc.scalar.copy(taper[:, part : part + PIECE], taper_banks[part][:])
+                        nc.vector.tensor_tensor(y[:, part : part + PIECE], raw[:, part : part + PIECE], taper_banks[part][:], MULT)
                 else:
                     nc.gpsimd.tensor_tensor(y[:, start : start + CHUNK], raw[:, start : start + CHUNK], taper[:, start : start + CHUNK], MULT)
             if block == 0:
+                nc.scalar.copy(taper[:, 0:PIECE], taper_banks[0][:])
                 nc.sync.dma_start(offsets[:], offs)
             windows.append(y)
 

@@ -69,18 +69,19 @@ def tile_tfft_kernel(tc, x, win, rw0, iw0, rw1, iw1, offs, out):
         make_identity(nc, identity[:])
         butterfly = make_butterfly(nc, held, identity, make_mix(nc, held, rw0, iw0, rw1, iw1))
 
-        win_quads = held.tile([P, S // P], F32, name="win_quads")
-        nc.sync.dma_start(
-            win_quads[:].rearrange("p (g e) -> p g e", e=QUAD),
-            win.rearrange("o (g p e) -> p (o g) e", p=P, e=QUAD),
-        )
+        rows = S // P
+        win_rows = held.tile([rows, P], F32, name="win_rows")
+        nc.sync.dma_start(win_rows[:], win.rearrange("o (g p) -> (o g) p", p=P))
+        flip_bank = banks.tile([P, PIECE], F32, name="mixed_bank")
+        nc.tensor.matmul(flip_bank[:, 0:rows], win_rows[:], identity[0:rows, 0:rows], start=True, stop=True)
+        win_columns = held.tile([P, rows], F32, name="win_columns")
+        nc.vector.tensor_copy(win_columns[:], flip_bank[:, 0:rows])
 
         def spread_taper(start):
             taper_bank = banks.tile([P, PIECE], F32, name="mixed_bank")
-            every_fourth = taper_bank[:].rearrange("c (p e) -> c p e", e=QUAD)
-            for e in range(QUAD):
-                column = QUAD * (start // PIECE) + e
-                nc.tensor.transpose(every_fourth[:, :, e], win_quads[:, column : column + 1].to_broadcast([P, P]), identity[:])
+            for part in range(0, PIECE, P):
+                column = (start + part) // P
+                nc.tensor.transpose(taper_bank[:, part : part + P], win_columns[:, column : column + 1].to_broadcast([P, P]), identity[:])
             return taper_bank
 
         offsets = held.tile([P, S // 16], U16, name="offsets")

@@ -11,6 +11,7 @@ C = 256
 S = 4096
 QUAD = 4
 PIECE = 512
+SLIVER = 128
 CHUNK = 512
 
 FLOPS = C * S * (1 + 2 * QUAD - 1)
@@ -59,10 +60,9 @@ def make_butterfly(nc, pool, identity, mix):
 def tile_tfft_kernel(tc, x, win, rw0, iw0, rw1, iw1, offs, out):
     nc = tc.nc
     blocks = C // P
-    pieces = [(block, piece) for block in range(blocks) for piece in range(S // PIECE)]
     with (
         tc.tile_pool(name="held", bufs=1) as held,
-        tc.tile_pool(name="work", bufs=4) as work,
+        tc.tile_pool(name="work", bufs=8) as work,
         tc.psum_pool(name="banks", bufs=8) as banks,
     ):
         identity = held.tile([P, P], F32, name="identity")
@@ -106,25 +106,32 @@ def tile_tfft_kernel(tc, x, win, rw0, iw0, rw1, iw1, offs, out):
                 nc.sync.dma_start(offsets[:], offs)
             windows.append(y)
 
-        def look_up_and_flip(block, piece):
+        def look_up_and_flip(block, first, cut):
             r0 = work.tile([P, PIECE], F32, name="r0", align_bytes=64)
-            listed = offsets[:, piece * (PIECE // 16) : (piece + 1) * (PIECE // 16)]
-            nc.scalar.activation(r0[:], windows[block][:].indirect(listed), COPY)
             flipped = work.tile([P, PIECE], F32, name="flipped", align_bytes=64)
-            nc.vector.transpose(flipped[:], r0[:])
+            for start in range(0, PIECE, cut):
+                listed = offsets[:, (first + start) // 16 : (first + start + cut) // 16]
+                nc.scalar.activation(r0[:, start : start + cut], windows[block][:].indirect(listed), COPY)
+                nc.vector.transpose(flipped[:, start : start + cut], r0[:, start : start + cut])
             return flipped
 
-        def mix_and_store(block, piece, flipped):
+        def mix_and_store(block, first, width, cut, flipped):
             mixed_bank = banks.tile([P, PIECE], F32, name="mixed_bank")
-            nc.tensor.matmul(mixed_bank[:], butterfly[:], flipped[:], start=True, stop=True)
+            for start in range(0, width, cut):
+                nc.tensor.matmul(mixed_bank[:, start : start + cut], butterfly[:], flipped[:, start : start + cut], start=True, stop=True)
             mixed = work.tile([P, PIECE], F32, name="mixed", align_bytes=64)
-            nc.vector.transpose(mixed[:], mixed_bank[:])
-            nc.sync.dma_start(out[block * P : (block + 1) * P, piece * PIECE : (piece + 1) * PIECE], mixed[:])
+            nc.vector.transpose(mixed[:, 0:width], mixed_bank[:, 0:width])
+            nc.sync.dma_start(out[block * P : (block + 1) * P, first : first + width], mixed[:, 0:width])
+
+        pieces = [(block, first) for block in range(blocks) for first in range(0, S, PIECE)]
 
         waiting = None
-        for block, piece in pieces:
-            flipped = look_up_and_flip(block, piece)
+        for piece in pieces:
+            cut = SLIVER if piece in (pieces[0], pieces[-1]) else PIECE
+            flipped = look_up_and_flip(*piece, cut)
             if waiting is not None:
                 mix_and_store(*waiting)
-            waiting = (block, piece, flipped)
-        mix_and_store(*waiting)
+            waiting = (*piece, PIECE, cut, flipped)
+        block, first = pieces[-1]
+        for start in range(0, PIECE, SLIVER):
+            mix_and_store(block, first + start, SLIVER, SLIVER, flipped[:, start : start + SLIVER])

@@ -12,7 +12,6 @@ S = 4096
 QUAD = 4
 PIECE = 512
 SLIVER = 128
-CHUNK = 512
 
 FLOPS = C * S * (1 + 2 * QUAD - 1)
 
@@ -62,6 +61,7 @@ def tile_tfft_kernel(tc, x, win, rw0, iw0, rw1, iw1, offs, out):
     blocks = C // P
     with (
         tc.tile_pool(name="held", bufs=1) as held,
+        tc.tile_pool(name="raws", bufs=S // PIECE) as raws,
         tc.tile_pool(name="work", bufs=8) as work,
         tc.psum_pool(name="banks", bufs=8) as banks,
     ):
@@ -85,26 +85,28 @@ def tile_tfft_kernel(tc, x, win, rw0, iw0, rw1, iw1, offs, out):
             return taper_bank
 
         offsets = held.tile([P, S // 16], U16, name="offsets")
-        taper = held.tile([P, S], F32, name="taper")
+        taper = held.tile([P, S - PIECE], F32, name="taper")
+        windows = [held.tile([P, S], F32, name="y" + str(block)) for block in range(blocks)]
         taper_banks = {}
-        windows = []
-        for block in range(blocks):
-            raw = held.tile([P, S], F32, name="raw" + str(block))
-            y = held.tile([P, S], F32, name="y" + str(block))
-            for start in range(0, S, CHUNK):
-                nc.sync.dma_start(raw[:, start : start + CHUNK], x[block * P : (block + 1) * P, start : start + CHUNK])
-                if block == 0:
-                    for part in range(start, start + CHUNK, PIECE):
-                        taper_banks[part] = spread_taper(part)
-                        if part > 0:
-                            nc.scalar.copy(taper[:, part : part + PIECE], taper_banks[part][:])
-                        nc.vector.tensor_tensor(y[:, part : part + PIECE], raw[:, part : part + PIECE], taper_banks[part][:], MULT)
-                else:
-                    nc.gpsimd.tensor_tensor(y[:, start : start + CHUNK], raw[:, start : start + CHUNK], taper[:, start : start + CHUNK], MULT)
-            if block == 0:
-                nc.scalar.copy(taper[:, 0:PIECE], taper_banks[0][:])
-                nc.sync.dma_start(offsets[:], offs)
-            windows.append(y)
+
+        def load_x(block, start):
+            raw = raws.tile([P, PIECE], F32, name="raw")
+            nc.sync.dma_start(raw[:], x[block * P : (block + 1) * P, start : start + PIECE])
+            return raw
+
+        for start in range(0, S, PIECE):
+            raw = load_x(0, start)
+            taper_banks[start] = spread_taper(start)
+            nc.vector.tensor_tensor(windows[0][:, start : start + PIECE], raw[:], taper_banks[start][:], MULT)
+            if start < S - PIECE:
+                nc.scalar.copy(taper[:, start : start + PIECE], taper_banks[start][:])
+        nc.sync.dma_start(offsets[:], offs)
+        for start in range(0, S, PIECE):
+            raw = load_x(1, start)
+            if start < S - PIECE:
+                nc.gpsimd.tensor_tensor(windows[1][:, start : start + PIECE], raw[:], taper[:, start : start + PIECE], MULT)
+            else:
+                nc.vector.tensor_tensor(windows[1][:, start : start + PIECE], raw[:], taper_banks[start][:], MULT)
 
         def look_up_and_flip(block, first, cut):
             r0 = work.tile([P, PIECE], F32, name="r0", align_bytes=64)

@@ -4,6 +4,7 @@ from concourse.masks import make_identity
 F32 = mybir.dt.float32
 U16 = mybir.dt.uint16
 MULT = mybir.AluOpType.mult
+ADD = mybir.AluOpType.add
 COPY = mybir.ActivationFunctionType.Copy
 
 P = 128
@@ -16,43 +17,48 @@ SLIVER = 128
 FLOPS = C * S * (1 + 2 * QUAD - 1)
 
 
-def load_for_all_partitions(queue, pool, source, name):
-    rows, cols = source.shape
-    tile = pool.tile([P, rows * cols], F32, name=name)
-    queue.dma_start(tile[:], source.rearrange("r c -> (r c)").partition_broadcast(P))
-    return tile
+def load_twiddles(nc, pool, rw0, iw0, rw1, iw1):
+    block = 8
+    twiddles = pool.tile([2, 4 * block], F32, name="twiddles")
+    for i, matrix in enumerate((rw1, iw1, rw0, iw0)):
+        nc.sync.dma_start(twiddles[:, i * block : i * block + matrix.shape[1]], matrix)
+    return twiddles[:].rearrange("r (i e) -> r i e", e=block)
 
 
-def make_mix(nc, pool, rw0, iw0, rw1, iw1):
-    stage_one = {"re": load_for_all_partitions(nc.sync, pool, rw0, "rw0_all"), "im": load_for_all_partitions(nc.scalar, pool, iw0, "iw0_all")}
-    stage_two = {"re": load_for_all_partitions(nc.sync, pool, rw1, "rw1_all"), "im": load_for_all_partitions(nc.scalar, pool, iw1, "iw1_all")}
-    products = {}
-    for part in ("re", "im"):
-        products[part] = pool.tile([P, QUAD * QUAD], F32, name="products_" + part)
-        by_a_b = products[part][:].rearrange("c (a b h q) -> c a b h q", a=2, b=2, h=2)
-        second = stage_two[part][:].rearrange("c (a h q) -> c a h q", a=2, h=2)
-        for b in range(2):
-            first = stage_one[part][:, 2 * b : 2 * b + 2].unsqueeze(1).unsqueeze(1).to_broadcast([P, 2, 2, 2])
-            nc.gpsimd.tensor_tensor(by_a_b[:, :, b, :, :], second, first, MULT)
-    mix = pool.tile([P, QUAD * QUAD], F32, name="mix")
-    nc.gpsimd.tensor_sub(mix[:], products["re"][:], products["im"][:])
-    return mix
+def make_butterfly(nc, pool, bank, identity, by_matrix):
+    spread_a = pool.tile([2, P], F32, name="spread_a")
+    nc.vector.tensor_copy(
+        spread_a[:].rearrange("r (u a b) -> r u a b", a=2, b=2),
+        identity[0:2, 0:2].unsqueeze(1).unsqueeze(3).to_broadcast([2, P // QUAD, 2, 2]),
+    )
+    spread_b = pool.tile([2, P], F32, name="spread_b")
+    nc.vector.tensor_copy(spread_b[:].rearrange("r (t b) -> r t b", b=2), identity[0:2, 0:2].unsqueeze(1).to_broadcast([2, P // 2, 2]))
 
+    nc.tensor.matmul(bank[:, 0:8], spread_a[:], by_matrix[:, 0:2, 0:4], start=True, stop=True)
+    nc.tensor.matmul(bank[:, 8:12], spread_b[:], by_matrix[:, 2:4, 0:2], start=True, stop=True)
+    rows_of_j = pool.tile([P, 12], F32, name="rows_of_j")
+    nc.vector.tensor_copy(rows_of_j[:], bank[:, 0:12])
 
-def make_butterfly(nc, pool, identity, mix):
+    products = pool.tile([P, 2 * QUAD], F32, name="products")
+    nc.gpsimd.tensor_tensor(
+        products[:].rearrange("j (i h q) -> j i h q", i=2, h=2),
+        rows_of_j[:, 0:8].rearrange("j (i h q) -> j i h q", i=2, h=2),
+        rows_of_j[:, 8:12].rearrange("j (i q) -> j i q", i=2).unsqueeze(2).to_broadcast([P, 2, 2, 2]),
+        MULT,
+    )
+    mix = pool.tile([P, QUAD], F32, name="mix")
+    nc.gpsimd.tensor_sub(mix[:], products[:, 0:QUAD], products[:, QUAD : 2 * QUAD])
+
     quads = P // QUAD
+    in_quad = pool.tile([P, quads], F32, name="in_quad")
+    nc.vector.tensor_reduce(out=in_quad[:], in_=identity[:].rearrange("j (u k) -> j u k", k=QUAD), op=ADD, axis=mybir.AxisListType.X)
     butterfly = pool.tile([P, P], F32, name="butterfly")
-    rows_of_tap = pool.tile([P, P], F32, name="rows_of_tap")
-    for k in range(QUAD):
-        target = butterfly if k == 0 else rows_of_tap
-        nc.gpsimd.tensor_tensor(
-            target[:].rearrange("j (u p) -> j u p", p=QUAD),
-            identity[:].rearrange("j (u k) -> j u k", k=QUAD)[:, :, k : k + 1].to_broadcast([P, quads, QUAD]),
-            mix[:, QUAD * k : QUAD * (k + 1)].unsqueeze(1).to_broadcast([P, quads, QUAD]),
-            MULT,
-        )
-        if k > 0:
-            nc.gpsimd.tensor_add(butterfly[:], butterfly[:], rows_of_tap[:])
+    nc.gpsimd.tensor_tensor(
+        butterfly[:].rearrange("j (u p) -> j u p", p=QUAD),
+        in_quad[:].unsqueeze(2).to_broadcast([P, quads, QUAD]),
+        mix[:].unsqueeze(1).to_broadcast([P, quads, QUAD]),
+        MULT,
+    )
     return butterfly
 
 
@@ -67,15 +73,18 @@ def tile_tfft_kernel(tc, x, win, rw0, iw0, rw1, iw1, offs, out):
     ):
         identity = held.tile([P, P], F32, name="identity")
         make_identity(nc, identity[:])
-        butterfly = make_butterfly(nc, held, identity, make_mix(nc, held, rw0, iw0, rw1, iw1))
 
         rows = S // P
         win_rows = held.tile([rows, P], F32, name="win_rows")
         nc.sync.dma_start(win_rows[:], win.rearrange("o (g p) -> (o g) p", p=P))
+        twiddles = load_twiddles(nc, held, rw0, iw0, rw1, iw1)
         flip_bank = banks.tile([P, PIECE], F32, name="mixed_bank")
         nc.tensor.matmul(flip_bank[:, 0:rows], win_rows[:], identity[0:rows, 0:rows], start=True, stop=True)
         win_columns = held.tile([P, rows], F32, name="win_columns")
         nc.vector.tensor_copy(win_columns[:], flip_bank[:, 0:rows])
+
+        twiddle_bank = banks.tile([P, PIECE], F32, name="mixed_bank")
+        butterfly = make_butterfly(nc, held, twiddle_bank, identity, twiddles)
 
         def spread_taper(start):
             taper_bank = banks.tile([P, PIECE], F32, name="mixed_bank")

@@ -12,6 +12,7 @@ C = 256
 S = 4096
 QUAD = 4
 PIECE = 512
+CHUNK = 1024
 SLIVER = 128
 
 FLOPS = C * S * (1 + 2 * QUAD - 1)
@@ -67,7 +68,7 @@ def tile_tfft_kernel(tc, x, win, rw0, iw0, rw1, iw1, offs, out):
     blocks = C // P
     with (
         tc.tile_pool(name="held", bufs=1) as held,
-        tc.tile_pool(name="raws", bufs=S // PIECE) as raws,
+        tc.tile_pool(name="raws", bufs=S // CHUNK) as raws,
         tc.tile_pool(name="work", bufs=8) as work,
         tc.psum_pool(name="banks", bufs=8) as banks,
     ):
@@ -98,24 +99,28 @@ def tile_tfft_kernel(tc, x, win, rw0, iw0, rw1, iw1, offs, out):
         windows = [held.tile([P, S], F32, name="y" + str(block)) for block in range(blocks)]
         taper_banks = {}
 
-        def load_x(block, start):
-            raw = raws.tile([P, PIECE], F32, name="raw")
-            nc.sync.dma_start(raw[:], x[block * P : (block + 1) * P, start : start + PIECE])
-            return raw
+        def load_x(block, chunk):
+            raw = raws.tile([P, CHUNK], F32, name="raw")
+            nc.sync.dma_start(raw[:], x[block * P : (block + 1) * P, chunk : chunk + CHUNK])
+            return {start: raw[:, start - chunk : start - chunk + PIECE] for start in range(chunk, chunk + CHUNK, PIECE)}
 
-        for start in range(0, S, PIECE):
-            raw = load_x(0, start)
-            taper_banks[start] = spread_taper(start)
-            nc.vector.tensor_tensor(windows[0][:, start : start + PIECE], raw[:], taper_banks[start][:], MULT)
-            if start < S - PIECE:
-                nc.scalar.copy(taper[:, start : start + PIECE], taper_banks[start][:])
+        for chunk in range(0, S, CHUNK):
+            for start, raw in load_x(0, chunk).items():
+                taper_banks[start] = spread_taper(start)
+                by_gpsimd = start == PIECE
+                if not by_gpsimd:
+                    nc.vector.tensor_tensor(windows[0][:, start : start + PIECE], raw, taper_banks[start][:], MULT)
+                if start < S - PIECE:
+                    nc.scalar.copy(taper[:, start : start + PIECE], taper_banks[start][:])
+                if by_gpsimd:
+                    nc.gpsimd.tensor_tensor(windows[0][:, start : start + PIECE], raw, taper[:, start : start + PIECE], MULT)
         nc.sync.dma_start(offsets[:], offs)
-        for start in range(0, S, PIECE):
-            raw = load_x(1, start)
-            if start < S - PIECE:
-                nc.gpsimd.tensor_tensor(windows[1][:, start : start + PIECE], raw[:], taper[:, start : start + PIECE], MULT)
-            else:
-                nc.vector.tensor_tensor(windows[1][:, start : start + PIECE], raw[:], taper_banks[start][:], MULT)
+        for chunk in range(0, S, CHUNK):
+            for start, raw in load_x(1, chunk).items():
+                if start < S - PIECE:
+                    nc.gpsimd.tensor_tensor(windows[1][:, start : start + PIECE], raw, taper[:, start : start + PIECE], MULT)
+                else:
+                    nc.vector.tensor_tensor(windows[1][:, start : start + PIECE], raw, taper_banks[start][:], MULT)
 
         def look_up_and_flip(block, first, cut):
             r0 = work.tile([P, PIECE], F32, name="r0", align_bytes=64)

import concourse.mybir as mybir
from concourse.masks import make_identity

F32 = mybir.dt.float32
U16 = mybir.dt.uint16
MULT = mybir.AluOpType.mult
ADD = mybir.AluOpType.add
COPY = mybir.ActivationFunctionType.Copy

P = 128
C = 256
S = 4096
QUAD = 4
PIECE = 512
CHUNK = 1024
SLIVER = 128

FLOPS = C * S * (1 + 2 * QUAD - 1)


def load_twiddles(nc, pool, rw0, iw0, rw1, iw1):
    block = 8
    twiddles = pool.tile([2, 4 * block], F32, name="twiddles")
    for i, matrix in enumerate((rw1, iw1, rw0, iw0)):
        nc.sync.dma_start(twiddles[:, i * block : i * block + matrix.shape[1]], matrix)
    return twiddles[:].rearrange("r (i e) -> r i e", e=block)


def make_butterfly(nc, pool, bank, identity, by_matrix):
    spread_a = pool.tile([2, P], F32, name="spread_a")
    nc.vector.tensor_copy(
        spread_a[:].rearrange("r (u a b) -> r u a b", a=2, b=2),
        identity[0:2, 0:2].unsqueeze(1).unsqueeze(3).to_broadcast([2, P // QUAD, 2, 2]),
    )
    spread_b = pool.tile([2, P], F32, name="spread_b")
    nc.vector.tensor_copy(spread_b[:].rearrange("r (t b) -> r t b", b=2), identity[0:2, 0:2].unsqueeze(1).to_broadcast([2, P // 2, 2]))

    nc.tensor.matmul(bank[:, 0:8], spread_a[:], by_matrix[:, 0:2, 0:4], start=True, stop=True)
    nc.tensor.matmul(bank[:, 8:12], spread_b[:], by_matrix[:, 2:4, 0:2], start=True, stop=True)
    rows_of_j = pool.tile([P, 12], F32, name="rows_of_j")
    nc.vector.tensor_copy(rows_of_j[:], bank[:, 0:12])

    products = pool.tile([P, 2 * QUAD], F32, name="products")
    nc.gpsimd.tensor_tensor(
        products[:].rearrange("j (i h q) -> j i h q", i=2, h=2),
        rows_of_j[:, 0:8].rearrange("j (i h q) -> j i h q", i=2, h=2),
        rows_of_j[:, 8:12].rearrange("j (i q) -> j i q", i=2).unsqueeze(2).to_broadcast([P, 2, 2, 2]),
        MULT,
    )
    mix = pool.tile([P, QUAD], F32, name="mix")
    nc.gpsimd.tensor_sub(mix[:], products[:, 0:QUAD], products[:, QUAD : 2 * QUAD])

    quads = P // QUAD
    in_quad = pool.tile([P, quads], F32, name="in_quad")
    nc.vector.tensor_reduce(out=in_quad[:], in_=identity[:].rearrange("j (u k) -> j u k", k=QUAD), op=ADD, axis=mybir.AxisListType.X)
    butterfly = pool.tile([P, P], F32, name="butterfly")
    nc.gpsimd.tensor_tensor(
        butterfly[:].rearrange("j (u p) -> j u p", p=QUAD),
        in_quad[:].unsqueeze(2).to_broadcast([P, quads, QUAD]),
        mix[:].unsqueeze(1).to_broadcast([P, quads, QUAD]),
        MULT,
    )
    return butterfly


def tile_tfft_kernel(tc, x, win, rw0, iw0, rw1, iw1, offs, out):
    nc = tc.nc
    blocks = C // P
    with (
        tc.tile_pool(name="held", bufs=1) as held,
        tc.tile_pool(name="raws", bufs=S // CHUNK) as raws,
        tc.tile_pool(name="work", bufs=8) as work,
        tc.psum_pool(name="banks", bufs=8) as banks,
    ):
        identity = held.tile([P, P], F32, name="identity")
        make_identity(nc, identity[:])

        rows = S // P
        win_rows = held.tile([rows, P], F32, name="win_rows")
        nc.sync.dma_start(win_rows[:], win.rearrange("o (g p) -> (o g) p", p=P))
        twiddles = load_twiddles(nc, held, rw0, iw0, rw1, iw1)
        flip_bank = banks.tile([P, PIECE], F32, name="mixed_bank")
        nc.tensor.matmul(flip_bank[:, 0:rows], win_rows[:], identity[0:rows, 0:rows], start=True, stop=True)
        win_columns = held.tile([P, rows], F32, name="win_columns")
        nc.vector.tensor_copy(win_columns[:], flip_bank[:, 0:rows])

        twiddle_bank = banks.tile([P, PIECE], F32, name="mixed_bank")
        butterfly = make_butterfly(nc, held, twiddle_bank, identity, twiddles)

        def spread_taper(start):
            taper_bank = banks.tile([P, PIECE], F32, name="mixed_bank")
            for part in range(0, PIECE, P):
                column = (start + part) // P
                nc.tensor.transpose(taper_bank[:, part : part + P], win_columns[:, column : column + 1].to_broadcast([P, P]), identity[:])
            return taper_bank

        offsets = held.tile([P, S // 16], U16, name="offsets")
        taper = held.tile([P, S - PIECE], F32, name="taper")
        windows = [held.tile([P, S], F32, name="y" + str(block)) for block in range(blocks)]
        taper_banks = {}

        def load_x(block, chunk):
            raw = raws.tile([P, CHUNK], F32, name="raw")
            nc.sync.dma_start(raw[:], x[block * P : (block + 1) * P, chunk : chunk + CHUNK])
            return {start: raw[:, start - chunk : start - chunk + PIECE] for start in range(chunk, chunk + CHUNK, PIECE)}

        for chunk in range(0, S, CHUNK):
            for start, raw in load_x(0, chunk).items():
                taper_banks[start] = spread_taper(start)
                by_gpsimd = start == PIECE
                if not by_gpsimd:
                    nc.vector.tensor_tensor(windows[0][:, start : start + PIECE], raw, taper_banks[start][:], MULT)
                if start < S - PIECE:
                    nc.scalar.copy(taper[:, start : start + PIECE], taper_banks[start][:])
                if by_gpsimd:
                    nc.gpsimd.tensor_tensor(windows[0][:, start : start + PIECE], raw, taper[:, start : start + PIECE], MULT)
        nc.sync.dma_start(offsets[:], offs)
        for chunk in range(0, S, CHUNK):
            for start, raw in load_x(1, chunk).items():
                if start < S - PIECE:
                    nc.gpsimd.tensor_tensor(windows[1][:, start : start + PIECE], raw, taper[:, start : start + PIECE], MULT)
                else:
                    nc.vector.tensor_tensor(windows[1][:, start : start + PIECE], raw, taper_banks[start][:], MULT)

        def look_up_and_flip(block, first, cut):
            r0 = work.tile([P, PIECE], F32, name="r0", align_bytes=64)
            flipped = work.tile([P, PIECE], F32, name="flipped", align_bytes=64)
            for start in range(0, PIECE, cut):
                listed = offsets[:, (first + start) // 16 : (first + start + cut) // 16]
                nc.scalar.activation(r0[:, start : start + cut], windows[block][:].indirect(listed), COPY)
                nc.vector.transpose(flipped[:, start : start + cut], r0[:, start : start + cut])
            return flipped

        def mix_and_store(block, first, width, cut, flipped):
            mixed_bank = banks.tile([P, PIECE], F32, name="mixed_bank")
            for start in range(0, width, cut):
                nc.tensor.matmul(mixed_bank[:, start : start + cut], butterfly[:], flipped[:, start : start + cut], start=True, stop=True)
            mixed = work.tile([P, PIECE], F32, name="mixed", align_bytes=64)
            nc.vector.transpose(mixed[:, 0:width], mixed_bank[:, 0:width])
            nc.sync.dma_start(out[block * P : (block + 1) * P, first : first + width], mixed[:, 0:width])

        pieces = [(block, first) for block in range(blocks) for first in range(0, S, PIECE)]

        waiting = None
        for piece in pieces:
            cut = SLIVER if piece in (pieces[0], pieces[-1]) else PIECE
            flipped = look_up_and_flip(*piece, cut)
            if waiting is not None:
                mix_and_store(*waiting)
            waiting = (*piece, PIECE, cut, flipped)
        block, first = pieces[-1]
        for start in range(0, PIECE, SLIVER):
            mix_and_store(block, first + start, SLIVER, SLIVER, flipped[:, start : start + SLIVER])
